import numpy as np
import ml_dtypes


def mxq(x, axis, fmt="e4m3"):
    dtype, down = {"e4m3": (ml_dtypes.float8_e4m3fn, 7), "e5m2": (ml_dtypes.float8_e5m2, 14)}[fmt]
    v = np.moveaxis(np.asarray(x, np.float32).astype(ml_dtypes.bfloat16).astype(np.float64), axis, -1)
    blocks = v.reshape(v.shape[:-1] + (-1, 32))
    amax = np.abs(blocks).max(-1, keepdims=True)
    byte = np.maximum(np.where(amax > 0, np.frexp(amax)[1] - 1 + 127, 0) - down, 1)
    scale = np.exp2(byte - 127.0)
    codes = (blocks / scale).astype(np.float32).astype(dtype).astype(np.float64)
    return np.moveaxis((codes * scale).reshape(v.shape), -1, axis)


WIDE = False


def mx_kscale(k):
    if not WIDE:
        return np.ones(k)
    levels = np.array([10, -10, 5, -5, 0])
    if k % 512:
        return np.exp2(np.random.permutation(np.resize(levels, k // 32))).repeat(32)
    a = np.empty((k // 512, 16))
    for p in range(k // 512):
        a[p, :8] = np.random.permutation(np.resize(levels, 8))
        for g in range(8):
            far = levels[np.abs(levels - a[p, g]) >= 10]
            a[p, g + 8] = far[np.random.randint(len(far))]
    return np.exp2(a.ravel()).repeat(32)


BF16 = ml_dtypes.bfloat16


def bf(x):
    return np.asarray(x, np.float32).astype(BF16)


def f64(x):
    return np.asarray(x).astype(np.float64)


B, G, DB, DR = 128, 16, 1024, 2048


def mish(v):
    return v * np.tanh(np.log(1.0 + np.exp(v)))


def setup_inputs():
    s, t = mx_kscale(DR), mx_kscale(DB)
    return {"BB_feature": bf(np.random.standard_normal((B, G, DB)) * t),
            "RF_feature": bf(np.random.standard_normal((B, DR)) * s),
            "W_bbbb": bf(np.random.standard_normal((DB, DB)) / np.sqrt(DB) / t),
            "b_bbbb": bf(np.random.standard_normal(DB) * 0.5),
            "W_rfbb": bf(np.random.standard_normal((DB, DR)) / np.sqrt(DR) / s),
            "b_rfbb": bf(np.random.standard_normal(DB) * 0.5)}


def reference(BB_feature, RF_feature, W_bbbb, b_bbbb, W_rfbb, b_rfbb):
    RF_to_BB = mish((mxq(f64(RF_feature), 1, "e4m3") @ mxq(f64(W_rfbb), 1, "e4m3").T) + f64(b_rfbb))
    BB_to_BB = mish((mxq(f64(BB_feature), 2, "e4m3") @ mxq(f64(W_bbbb), 1, "e4m3").T) + f64(b_bbbb))
    return BB_to_BB + RF_to_BB[:, None, :]

@@ -1,0 +1,271 @@
+from contextlib import ExitStack
+
+import concourse.mybir as mybir
+from concourse.masks import make_identity
+
+F32 = mybir.dt.float32
+BF16 = mybir.dt.bfloat16
+U32 = mybir.dt.uint32
+U8 = mybir.dt.uint8
+FP8X4 = mybir.dt.float8_e4m3fn_x4
+FUNC = mybir.ActivationFunctionType
+ALU = mybir.AluOpType
+
+P = 128
+GROUPS = 16
+D_BB = 1024
+D_RF = 2048
+K_PASS = 512
+HALF = 512
+BATCH = 4096
+CHUNK = 4
+BLOCKS_PER_BANK = 4
+TINY = 2.0 ** -60
+
+FLOPS = 2 * P * GROUPS * D_BB * D_BB + 2 * P * D_RF * D_BB
+
+
+def tile_gnn_layer_pb_kernel(tc, BB_feature, RF_feature, W_bbbb, b_bbbb, W_rfbb, b_rfbb, out):
+    nc = tc.nc
+    with ExitStack() as stack:
+        const = stack.enter_context(tc.tile_pool(name="const", bufs=1))
+        raw_pool = stack.enter_context(tc.tile_pool(name="raw", bufs=4))
+        grouped_pool = stack.enter_context(tc.tile_pool(name="grouped", bufs=3))
+        keep = stack.enter_context(tc.tile_pool(name="keep", bufs=1))
+        turn = stack.enter_context(tc.tile_pool(name="turn", bufs=3))
+        work = stack.enter_context(tc.tile_pool(name="work", bufs=1))
+        flip_psum = stack.enter_context(tc.psum_pool(name="flip", bufs=4))
+        acc_psum = stack.enter_context(tc.psum_pool(name="acc", bufs=4))
+        stack.enter_context(tc.manual_schedule())
+
+        def load(view, row_tiles):
+            raw = raw_pool.tile([P, BATCH], BF16, name="raw")
+            cols = view.shape[-1] * row_tiles
+            nc.sync.dma_start(out=raw[:, :cols].rearrange("p (j k) -> p j k", j=row_tiles), in_=view)
+            return raw
+
+        def x_view(q):
+            return BB_feature[:, q * CHUNK : (q + 1) * CHUNK, :]
+
+        def w_view(weight, first_row, row_tiles):
+            return weight[first_row : first_row + row_tiles * P, :].rearrange("(j p) k -> p j k", p=P)
+
+        raw_wbb0 = load(w_view(W_bbbb, 0, 4), 4)
+        raw_x0 = load(x_view(0), CHUNK)
+        bias_rows = const.tile([P, 2 * D_BB], BF16, name="bias_rows")
+        nc.vector.memset(bias_rows[:], 0.0)
+        nc.sync.dma_start(out=bias_rows[0:1, :D_BB], in_=b_bbbb.rearrange("(o n) -> o n", o=1))
+        nc.sync.dma_start(out=bias_rows[0:1, D_BB:], in_=b_rfbb.rearrange("(o n) -> o n", o=1))
+        raw_wbb1 = load(w_view(W_bbbb, HALF, 4), 4)
+        raw_x1 = load(x_view(1), CHUNK)
+
+        ident = const.tile([P, P], F32, name="ident")
+        make_identity(nc, ident[:])
+        tiny = const.tile([P, 1], F32, name="tiny")
+        nc.vector.memset(tiny[:], TINY)
+        warm = const.tile([P, 1], F32, name="warm")
+
+        ones = const.tile([P, P], BF16, name="ones")
+        nc.vector.memset(ones[:], 1.0)
+        bias_bb = const.tile([P, D_BB], BF16, name="bias_bb")
+        bias_rf = const.tile([P, D_BB], BF16, name="bias_rf")
+
+        def load_sigmoid_table():
+            nc.scalar.activation(out=warm[:], in_=tiny[:], func=FUNC.Sigmoid)
+
+        load_sigmoid_table()
+
+        def spread_bias(spread, first):
+            for h in range(D_BB // HALF):
+                row = bias_rows[:, first + h * HALF : first + (h + 1) * HALF]
+                acc = acc_psum.tile([P, HALF], F32, name="acc")
+                nc.tensor.matmul(out=acc[:], lhsT=ones[:], rhs=row, start=True, stop=True)
+                nc.vector.tensor_copy(out=spread[:, h * HALF : (h + 1) * HALF], in_=acc[:])
+
+        z = [work.tile([P, D_BB], F32, name="z%d" % g) for g in range(GROUPS + 1)]
+        w = [work.tile([P, D_BB], F32, name="w%d" % g) for g in range(GROUPS + 1)]
+        RF = GROUPS
+
+        def flip(raw, blocks):
+            words = raw[:].bitcast(F32)
+            banks = []
+            for first in range(0, blocks, BLOCKS_PER_BANK):
+                bank = flip_psum.tile([P, BLOCKS_PER_BANK, P], F32, name="bank")
+                for s in range(BLOCKS_PER_BANK):
+                    n = first + s
+                    pair = n // 2 * 2 * P
+                    nc.tensor.transpose(bank[:, s, :], words[:, pair + n % 2 : pair + 2 * P : 2], ident[:])
+                banks.append(bank)
+            return banks
+
+        def regroup(banks, passes, row_tiles, scalar_banks):
+            grouped = grouped_pool.tile([P, BATCH], BF16, name="grouped", align_bytes=64)
+            cols = passes * row_tiles * P * 4
+            pairs = grouped[:, :cols].bitcast(F32).rearrange(
+                "p (c j r u) -> p c j r u", c=passes, j=row_tiles, u=2
+            )
+            banks_per_row_tile = passes // 2
+            for k, bank in enumerate(banks):
+                j, h = divmod(k, banks_per_row_tile)
+                dst = pairs[:, 2 * h : 2 * h + 2, j]
+                src = bank[:].rearrange("p (c u) r -> p c r u", u=2)
+                if k >= len(banks) - scalar_banks:
+                    nc.scalar.copy(out=dst, in_=src)
+                else:
+                    nc.vector.tensor_copy(out=dst, in_=src)
+            return grouped[:, :cols]
+
+        def quantise(grouped, pool, tag):
+            words = grouped.shape[-1] // 4
+            codes = pool.tile([P, words], U32, name="codes_" + tag, align_bytes=64)
+            scales = pool.tile([P, words], U8, name="scales_" + tag, align_bytes=64)
+            nc.vector.quantize_mx(out=codes[:].bitcast(FP8X4), scales=scales[:], in_=grouped)
+            return codes, scales
+
+        def product(acc, stationary, j, row_tiles, moving, width, passes):
+            s_codes, s_scales = stationary
+            m_codes, m_scales = moving
+            for c in range(passes):
+                s_cols = slice((c * row_tiles + j) * P, (c * row_tiles + j + 1) * P)
+                m_cols = slice(c * width, (c + 1) * width)
+                nc.tensor.matmul_mx(
+                    out=acc,
+                    lhsT=s_codes[:, s_cols].bitcast(FP8X4),
+                    lhsT_scale=s_scales[:, s_cols],
+                    rhs=m_codes[:, m_cols].bitcast(FP8X4),
+                    rhs_scale=m_scales[:, m_cols],
+                    start=(c == 0),
+                    stop=(c == passes - 1),
+                )
+
+        w_bb = [None, None]
+
+        def multiply_bb(x_mx, g, h):
+            acc = acc_psum.tile([P, HALF], F32, name="acc")
+            product(acc[:], x_mx, g % CHUNK, CHUNK, w_bb[h], HALF, D_BB // K_PASS)
+            cols = slice(h * HALF, (h + 1) * HALF)
+            nc.vector.tensor_tensor(out=z[g][:, cols], in0=acc[:], in1=bias_bb[:, cols], op=ALU.add)
+
+        def sigmoid(g, cols=slice(0, D_BB)):
+            nc.scalar.activation(out=w[g][:, cols], in_=z[g][:, cols], func=FUNC.Sigmoid, scale=-1.0)
+
+        def log(g):
+            nc.scalar.activation(out=w[g][:], in_=w[g][:], func=FUNC.Ln, bias=tiny[:])
+
+        def tanh(g):
+            nc.scalar.activation(out=w[g][:], in_=w[g][:], func=FUNC.Tanh, scale=-1.0)
+
+        def times_z(engine, g):
+            engine.tensor_tensor(out=w[g][:], in0=z[g][:], in1=w[g][:], op=ALU.mult)
+
+        def park(values, pool, name):
+            banks = []
+            for h in range(D_BB // HALF):
+                bank = pool.tile([P, HALF], F32, name=name)
+                nc.tensor.matmul(out=bank[:], lhsT=ident[:], rhs=values[:, h * HALF : (h + 1) * HALF], start=True, stop=True)
+                banks.append(bank)
+            return banks
+
+        def with_parked(g, banks, op):
+            for h in range(D_BB // HALF):
+                cols = slice(h * HALF, (h + 1) * HALF)
+                nc.vector.tensor_tensor(out=w[g][:, cols], in0=banks[h][:], in1=w[g][:, cols], op=op)
+
+        def finish(g):
+            with_parked(g, rf_banks, ALU.add)
+            nc.sync.dma_start(out=out[:, g, :], in_=w[g][:])
+
+        g_wbb0 = regroup(flip(raw_wbb0, 16), 2, 4, 2)
+        raw_x2 = load(x_view(2), CHUNK)
+        w_bb[0] = quantise(g_wbb0, keep, "wbb0")
+        g_x0 = regroup(flip(raw_x0, 16), 2, CHUNK, 2)
+        raw_rf = load(RF_feature.rearrange("b (j k) -> b j k", j=1), 1)
+        x0 = quantise(g_x0, turn, "turn")
+        spread_bias(bias_bb, 0)
+        g_wbb1 = regroup(flip(raw_wbb1, 16), 2, 4, 4)
+        raw_wrf = [load(w_view(W_rfbb, 0, 2), 2)]
+        for g in range(0, CHUNK // 2):
+            multiply_bb(x0, g, 0)
+            sigmoid(g, slice(0, HALF))
+        w_bb[1] = quantise(g_wbb1, keep, "wbb1")
+        for g in range(CHUNK // 2, CHUNK):
+            multiply_bb(x0, g, 0)
+            sigmoid(g, slice(0, HALF))
+        banks_x1 = flip(raw_x1, 16)
+        raw_wrf.append(load(w_view(W_rfbb, 2 * P, 2), 2))
+        g_x1 = regroup(banks_x1, 2, CHUNK, 4)
+        for g in range(0, CHUNK):
+            multiply_bb(x0, g, 1)
+            sigmoid(g, slice(HALF, D_BB))
+
+        banks_x2 = flip(raw_x2, 16)
+        x1 = quantise(g_x1, turn, "turn")
+        g_x2 = regroup(banks_x2, 2, CHUNK, 2)
+        raw_wrf.append(load(w_view(W_rfbb, 4 * P, 2), 2))
+        for g in range(CHUNK, 2 * CHUNK):
+            multiply_bb(x1, g, 0)
+            multiply_bb(x1, g, 1)
+            sigmoid(g)
+        x2 = quantise(g_x2, turn, "turn")
+        for g in range(0, 2 * CHUNK):
+            log(g)
+
+        spread_bias(bias_rf, D_BB)
+        g_rf = regroup(flip(raw_rf, 8), 4, 1, 0)
+        raw_wrf.append(load(w_view(W_rfbb, 6 * P, 2), 2))
+        g_wrf = regroup(flip(raw_wrf[0], 16), 4, 2, 0)
+        raw_x3 = load(x_view(3), CHUNK)
+        for g in range(2 * CHUNK, 3 * CHUNK):
+            multiply_bb(x2, g, 0)
+            multiply_bb(x2, g, 1)
+            sigmoid(g)
+        rf_mx = quantise(g_rf, keep, "rf")
+        wrf_mx = quantise(g_wrf, turn, "turn")
+        for g in range(0, 2 * CHUNK):
+            tanh(g)
+            times_z(nc.gpsimd, g)
+
+        WIDTH_RF = 2 * P
+        for i in range(4):
+            if i < 3:
+                g_next = regroup(flip(raw_wrf[i + 1], 16), 4, 2, 0)
+            acc = acc_psum.tile([P, HALF], F32, name="acc")
+            product(acc[:, :WIDTH_RF], rf_mx, 0, 1, wrf_mx, WIDTH_RF, D_RF // K_PASS)
+            cols = slice(i * WIDTH_RF, (i + 1) * WIDTH_RF)
+            nc.vector.tensor_tensor(out=z[RF][:, cols], in0=acc[:, :WIDTH_RF], in1=bias_rf[:, cols], op=ALU.add)
+            if i < 3:
+                wrf_mx = quantise(g_next, turn, "turn")
+        sigmoid(RF)
+        z_rf_banks = park(z[RF], flip_psum, "bank")
+        x3 = quantise(regroup(flip(raw_x3, 16), 2, CHUNK, 0), turn, "turn")
+
+        log(RF)
+        for g in range(2 * CHUNK, 3 * CHUNK):
+            log(g)
+        for g in range(3 * CHUNK, GROUPS):
+            multiply_bb(x3, g, 0)
+            multiply_bb(x3, g, 1)
+
+        load_sigmoid_table()
+        tanh(RF)
+        with_parked(RF, z_rf_banks, ALU.mult)
+        rf_banks = park(w[RF], flip_psum, "bank")
+        for g in range(0, 2 * CHUNK):
+            finish(g)
+        for g in range(3 * CHUNK, GROUPS):
+            sigmoid(g)
+
+        for g in range(2 * CHUNK, 3 * CHUNK):
+            tanh(g)
+            times_z(nc.gpsimd, g)
+            finish(g)
+        for g in range(3 * CHUNK, GROUPS):
+            log(g)
+        z_banks = [park(z[g], acc_psum, "acc") for g in range(3 * CHUNK + 1, GROUPS, 2)]
+        for g in range(3 * CHUNK, GROUPS, 2):
+            tanh(g)
+            times_z(nc.gpsimd, g)
+            tanh(g + 1)
+            with_parked(g + 1, z_banks[(g - 3 * CHUNK) // 2], ALU.mult)
+            finish(g + 1)
+            finish(g)

@@ -15,10 +15,9 @@ P = 128
 GROUPS = 16
 D_BB = 1024
 D_RF = 2048
-K_PASS = 512
 HALF = 512
-BATCH = 4096
-CHUNK = 4
+PIECE = 2048
+WORDS = PIECE // 4
 BLOCKS_PER_BANK = 4
 TINY = 2.0 ** -60
 
@@ -29,42 +28,49 @@ def tile_gnn_layer_pb_kernel(tc, BB_feature, RF_feature, W_bbbb, b_bbbb, W_rfbb,
     nc = tc.nc
     with ExitStack() as stack:
         const = stack.enter_context(tc.tile_pool(name="const", bufs=1))
-        raw_pool = stack.enter_context(tc.tile_pool(name="raw", bufs=4))
-        grouped_pool = stack.enter_context(tc.tile_pool(name="grouped", bufs=3))
+        raw_pool = stack.enter_context(tc.tile_pool(name="raw", bufs=10))
+        grouped_pool = stack.enter_context(tc.tile_pool(name="grouped", bufs=5))
         keep = stack.enter_context(tc.tile_pool(name="keep", bufs=1))
-        turn = stack.enter_context(tc.tile_pool(name="turn", bufs=3))
+        turn = stack.enter_context(tc.tile_pool(name="turn", bufs=6))
         work = stack.enter_context(tc.tile_pool(name="work", bufs=1))
         flip_psum = stack.enter_context(tc.psum_pool(name="flip", bufs=4))
         acc_psum = stack.enter_context(tc.psum_pool(name="acc", bufs=4))
         stack.enter_context(tc.manual_schedule())
 
-        def load(view, row_tiles):
-            raw = raw_pool.tile([P, BATCH], BF16, name="raw")
-            cols = view.shape[-1] * row_tiles
-            nc.sync.dma_start(out=raw[:, :cols].rearrange("p (j k) -> p j k", j=row_tiles), in_=view)
-            return raw
+        views = {"rf": RF_feature.rearrange("b (j k) -> b j k", j=1)}
+        for i in range(4):
+            views["w%d" % i] = W_bbbb[2 * P * i : 2 * P * (i + 1), :].rearrange("(j p) k -> p j k", p=P)
+        for i in range(8):
+            views["x%d" % i] = BB_feature[:, 2 * i : 2 * i + 2, :]
+            views["r%d" % i] = W_rfbb[P * i : P * (i + 1), :].rearrange("(j p) k -> p j k", p=P)
+        to_load = ["w0", "x0", "w1", "x1", "w2", "w3", "x2", "x3", "rf"]
+        to_load += ["r%d" % i for i in range(8)] + ["x4", "x5", "x6", "x7"]
+        raw = {}
+        grouped = {}
+        mx = {}
 
-        def x_view(q):
-            return BB_feature[:, q * CHUNK : (q + 1) * CHUNK, :]
+        def load():
+            if to_load:
+                name = to_load[0]
+                to_load.remove(name)
+                raw[name] = raw_pool.tile([P, PIECE], BF16, name="raw")
+                view = views[name]
+                nc.sync.dma_start(out=raw[name][:].rearrange("p (j k) -> p j k", j=view.shape[1]), in_=view)
 
-        def w_view(weight, first_row, row_tiles):
-            return weight[first_row : first_row + row_tiles * P, :].rearrange("(j p) k -> p j k", p=P)
-
-        raw_wbb0 = load(w_view(W_bbbb, 0, 4), 4)
-        raw_x0 = load(x_view(0), CHUNK)
         bias_rows = const.tile([P, 2 * D_BB], BF16, name="bias_rows")
-        nc.vector.memset(bias_rows[:], 0.0)
+        nc.vector.memset(bias_rows[:].bitcast(U32), 0)
+        for i in range(2):
+            load()
         nc.sync.dma_start(out=bias_rows[0:1, :D_BB], in_=b_bbbb.rearrange("(o n) -> o n", o=1))
         nc.sync.dma_start(out=bias_rows[0:1, D_BB:], in_=b_rfbb.rearrange("(o n) -> o n", o=1))
-        raw_wbb1 = load(w_view(W_bbbb, HALF, 4), 4)
-        raw_x1 = load(x_view(1), CHUNK)
+        for i in range(8):
+            load()
 
         ident = const.tile([P, P], F32, name="ident")
         make_identity(nc, ident[:])
         tiny = const.tile([P, 1], F32, name="tiny")
         nc.vector.memset(tiny[:], TINY)
         warm = const.tile([P, 1], F32, name="warm")
-
         ones = const.tile([P, P], BF16, name="ones")
         nc.vector.memset(ones[:], 1.0)
         bias_bb = const.tile([P, D_BB], BF16, name="bias_bb")
@@ -80,51 +86,45 @@ def tile_gnn_layer_pb_kernel(tc, BB_feature, RF_feature, W_bbbb, b_bbbb, W_rfbb,
                 row = bias_rows[:, first + h * HALF : first + (h + 1) * HALF]
                 acc = acc_psum.tile([P, HALF], F32, name="acc")
                 nc.tensor.matmul(out=acc[:], lhsT=ones[:], rhs=row, start=True, stop=True)
-                nc.vector.tensor_copy(out=spread[:, h * HALF : (h + 1) * HALF], in_=acc[:])
+                nc.scalar.copy(out=spread[:, h * HALF : (h + 1) * HALF], in_=acc[:])
 
         z = [work.tile([P, D_BB], F32, name="z%d" % g) for g in range(GROUPS + 1)]
         w = [work.tile([P, D_BB], F32, name="w%d" % g) for g in range(GROUPS + 1)]
         RF = GROUPS
 
-        def flip(raw, blocks):
-            words = raw[:].bitcast(F32)
-            banks = []
-            for first in range(0, blocks, BLOCKS_PER_BANK):
-                bank = flip_psum.tile([P, BLOCKS_PER_BANK, P], F32, name="bank")
-                for s in range(BLOCKS_PER_BANK):
-                    n = first + s
-                    pair = n // 2 * 2 * P
-                    nc.tensor.transpose(bank[:, s, :], words[:, pair + n % 2 : pair + 2 * P : 2], ident[:])
-                banks.append(bank)
-            return banks
-
-        def regroup(banks, passes, row_tiles, scalar_banks):
-            grouped = grouped_pool.tile([P, BATCH], BF16, name="grouped", align_bytes=64)
-            cols = passes * row_tiles * P * 4
-            pairs = grouped[:, :cols].bitcast(F32).rearrange(
+        def flip(name, copies):
+            words = raw[name][:].bitcast(F32)
+            row_tiles = views[name].shape[1]
+            passes = 4 // row_tiles
+            grouped[name] = grouped_pool.tile([P, PIECE], BF16, name="grouped", align_bytes=64)
+            pairs = grouped[name][:].bitcast(F32).rearrange(
                 "p (c j r u) -> p c j r u", c=passes, j=row_tiles, u=2
             )
-            banks_per_row_tile = passes // 2
-            for k, bank in enumerate(banks):
-                j, h = divmod(k, banks_per_row_tile)
-                dst = pairs[:, 2 * h : 2 * h + 2, j]
+            for b in range(2):
+                bank = flip_psum.tile([P, BLOCKS_PER_BANK, P], F32, name="bank")
+                for s in range(BLOCKS_PER_BANK):
+                    n = BLOCKS_PER_BANK * b + s
+                    pair = n // 2 * 2 * P
+                    nc.tensor.transpose(bank[:, s, :], words[:, pair + n % 2 : pair + 2 * P : 2], ident[:])
+                dst = pairs[:, 0:2, b] if row_tiles == 2 else pairs[:, 2 * b : 2 * b + 2, 0]
                 src = bank[:].rearrange("p (c u) r -> p c r u", u=2)
-                if k >= len(banks) - scalar_banks:
+                if copies[b] == "S":
                     nc.scalar.copy(out=dst, in_=src)
                 else:
                     nc.vector.tensor_copy(out=dst, in_=src)
-            return grouped[:, :cols]
+            load()
 
-        def quantise(grouped, pool, tag):
-            words = grouped.shape[-1] // 4
-            codes = pool.tile([P, words], U32, name="codes_" + tag, align_bytes=64)
-            scales = pool.tile([P, words], U8, name="scales_" + tag, align_bytes=64)
-            nc.vector.quantize_mx(out=codes[:].bitcast(FP8X4), scales=scales[:], in_=grouped)
-            return codes, scales
+        def quantise(name):
+            pool = turn if name[0] == "x" or (name[0] == "r" and name != "rf") else keep
+            tag = "turn" if pool is turn else name
+            codes = pool.tile([P, WORDS], U32, name="codes_" + tag, align_bytes=64)
+            scales = pool.tile([P, WORDS], U8, name="scales_" + tag, align_bytes=64)
+            nc.vector.quantize_mx(out=codes[:].bitcast(FP8X4), scales=scales[:], in_=grouped[name][:])
+            mx[name] = (codes, scales)
 
         def product(acc, stationary, j, row_tiles, moving, width, passes):
-            s_codes, s_scales = stationary
-            m_codes, m_scales = moving
+            s_codes, s_scales = mx[stationary]
+            m_codes, m_scales = mx[moving]
             for c in range(passes):
                 s_cols = slice((c * row_tiles + j) * P, (c * row_tiles + j + 1) * P)
                 m_cols = slice(c * width, (c + 1) * width)
@@ -138,13 +138,24 @@ def tile_gnn_layer_pb_kernel(tc, BB_feature, RF_feature, W_bbbb, b_bbbb, W_rfbb,
                     stop=(c == passes - 1),
                 )
 
-        w_bb = [None, None]
-
-        def multiply_bb(x_mx, g, h):
+        def multiply_bb(g, h):
             acc = acc_psum.tile([P, HALF], F32, name="acc")
-            product(acc[:], x_mx, g % CHUNK, CHUNK, w_bb[h], HALF, D_BB // K_PASS)
+            for i in range(2):
+                product(acc[:, 2 * P * i : 2 * P * (i + 1)], "x%d" % (g // 2), g % 2, 2, "w%d" % (2 * h + i), 2 * P, 2)
             cols = slice(h * HALF, (h + 1) * HALF)
             nc.vector.tensor_tensor(out=z[g][:, cols], in0=acc[:], in1=bias_bb[:, cols], op=ALU.add)
+
+        rf_acc = []
+
+        def multiply_rf(i):
+            if i % 4 == 0:
+                acc = acc_psum.tile([P, HALF], F32, name="acc")
+                rf_acc.append(acc)
+            acc = rf_acc[i // 4]
+            product(acc[:, P * (i % 4) : P * (i % 4 + 1)], "rf", 0, 1, "r%d" % i, P, 4)
+            if i % 4 == 3:
+                cols = slice(i // 4 * HALF, (i // 4 + 1) * HALF)
+                nc.vector.tensor_tensor(out=z[RF][:, cols], in0=acc[:], in1=bias_rf[:, cols], op=ALU.add)
 
         def sigmoid(g, cols=slice(0, D_BB)):
             nc.scalar.activation(out=w[g][:, cols], in_=z[g][:, cols], func=FUNC.Sigmoid, scale=-1.0)
@@ -155,117 +166,132 @@ def tile_gnn_layer_pb_kernel(tc, BB_feature, RF_feature, W_bbbb, b_bbbb, W_rfbb,
         def tanh(g):
             nc.scalar.activation(out=w[g][:], in_=w[g][:], func=FUNC.Tanh, scale=-1.0)
 
-        def times_z(engine, g):
-            engine.tensor_tensor(out=w[g][:], in0=z[g][:], in1=w[g][:], op=ALU.mult)
+        def times_z(g):
+            nc.gpsimd.tensor_tensor(out=w[g][:], in0=z[g][:], in1=w[g][:], op=ALU.mult)
 
-        def park(values, pool, name):
-            banks = []
-            for h in range(D_BB // HALF):
-                bank = pool.tile([P, HALF], F32, name=name)
-                nc.tensor.matmul(out=bank[:], lhsT=ident[:], rhs=values[:, h * HALF : (h + 1) * HALF], start=True, stop=True)
-                banks.append(bank)
-            return banks
+        def park(values, h, pool, name):
+            bank = pool.tile([P, HALF], F32, name=name)
+            nc.tensor.matmul(out=bank[:], lhsT=ident[:], rhs=values[:, h * HALF : (h + 1) * HALF], start=True, stop=True)
+            return bank
 
         def with_parked(g, banks, op):
             for h in range(D_BB // HALF):
                 cols = slice(h * HALF, (h + 1) * HALF)
                 nc.vector.tensor_tensor(out=w[g][:, cols], in0=banks[h][:], in1=w[g][:, cols], op=op)
 
+        def store(g, cols=slice(0, D_BB)):
+            nc.sync.dma_start(out=out[:, g, cols], in_=w[g][:, cols])
+
         def finish(g):
             with_parked(g, rf_banks, ALU.add)
-            nc.sync.dma_start(out=out[:, g, :], in_=w[g][:])
+            store(g)
 
-        g_wbb0 = regroup(flip(raw_wbb0, 16), 2, 4, 2)
-        raw_x2 = load(x_view(2), CHUNK)
-        w_bb[0] = quantise(g_wbb0, keep, "wbb0")
-        g_x0 = regroup(flip(raw_x0, 16), 2, CHUNK, 2)
-        raw_rf = load(RF_feature.rearrange("b (j k) -> b j k", j=1), 1)
-        x0 = quantise(g_x0, turn, "turn")
+        first = slice(0, HALF)
+        second = slice(HALF, D_BB)
+
+        flip("w0", "VS")
+        flip("x0", "VS")
+        quantise("w0")
+        quantise("x0")
+        flip("w1", "SS")
+        quantise("w1")
         spread_bias(bias_bb, 0)
-        g_wbb1 = regroup(flip(raw_wbb1, 16), 2, 4, 4)
-        raw_wrf = [load(w_view(W_rfbb, 0, 2), 2)]
-        for g in range(0, CHUNK // 2):
-            multiply_bb(x0, g, 0)
-            sigmoid(g, slice(0, HALF))
-        w_bb[1] = quantise(g_wbb1, keep, "wbb1")
-        for g in range(CHUNK // 2, CHUNK):
-            multiply_bb(x0, g, 0)
-            sigmoid(g, slice(0, HALF))
-        banks_x1 = flip(raw_x1, 16)
-        raw_wrf.append(load(w_view(W_rfbb, 2 * P, 2), 2))
-        g_x1 = regroup(banks_x1, 2, CHUNK, 4)
-        for g in range(0, CHUNK):
-            multiply_bb(x0, g, 1)
-            sigmoid(g, slice(HALF, D_BB))
-
-        banks_x2 = flip(raw_x2, 16)
-        x1 = quantise(g_x1, turn, "turn")
-        g_x2 = regroup(banks_x2, 2, CHUNK, 2)
-        raw_wrf.append(load(w_view(W_rfbb, 4 * P, 2), 2))
-        for g in range(CHUNK, 2 * CHUNK):
-            multiply_bb(x1, g, 0)
-            multiply_bb(x1, g, 1)
-            sigmoid(g)
-        x2 = quantise(g_x2, turn, "turn")
-        for g in range(0, 2 * CHUNK):
-            log(g)
-
+        flip("x1", "VS")
+        for g in (0, 1):
+            multiply_bb(g, 0)
+        for g in (0, 1):
+            sigmoid(g, first)
+        quantise("x1")
+        flip("w2", "VS")
+        flip("w3", "VS")
+        for g in (2, 3):
+            multiply_bb(g, 0)
+        for g in (2, 3):
+            sigmoid(g, first)
+        quantise("w2")
+        quantise("w3")
+        flip("x2", "SS")
+        flip("x3", "SV")
+        for g in (0, 1):
+            multiply_bb(g, 1)
+            sigmoid(g, second)
+        quantise("x2")
         spread_bias(bias_rf, D_BB)
-        g_rf = regroup(flip(raw_rf, 8), 4, 1, 0)
-        raw_wrf.append(load(w_view(W_rfbb, 6 * P, 2), 2))
-        g_wrf = regroup(flip(raw_wrf[0], 16), 4, 2, 0)
-        raw_x3 = load(x_view(3), CHUNK)
-        for g in range(2 * CHUNK, 3 * CHUNK):
-            multiply_bb(x2, g, 0)
-            multiply_bb(x2, g, 1)
+        for g in (2, 3):
+            multiply_bb(g, 1)
+            sigmoid(g, second)
+        quantise("x3")
+        for g in range(4, 8):
+            multiply_bb(g, 0)
+            multiply_bb(g, 1)
             sigmoid(g)
-        rf_mx = quantise(g_rf, keep, "rf")
-        wrf_mx = quantise(g_wrf, turn, "turn")
-        for g in range(0, 2 * CHUNK):
-            tanh(g)
-            times_z(nc.gpsimd, g)
-
-        WIDTH_RF = 2 * P
-        for i in range(4):
-            if i < 3:
-                g_next = regroup(flip(raw_wrf[i + 1], 16), 4, 2, 0)
-            acc = acc_psum.tile([P, HALF], F32, name="acc")
-            product(acc[:, :WIDTH_RF], rf_mx, 0, 1, wrf_mx, WIDTH_RF, D_RF // K_PASS)
-            cols = slice(i * WIDTH_RF, (i + 1) * WIDTH_RF)
-            nc.vector.tensor_tensor(out=z[RF][:, cols], in0=acc[:, :WIDTH_RF], in1=bias_rf[:, cols], op=ALU.add)
-            if i < 3:
-                wrf_mx = quantise(g_next, turn, "turn")
-        sigmoid(RF)
-        z_rf_banks = park(z[RF], flip_psum, "bank")
-        x3 = quantise(regroup(flip(raw_x3, 16), 2, CHUNK, 0), turn, "turn")
-
-        log(RF)
-        for g in range(2 * CHUNK, 3 * CHUNK):
+        flip("rf", "VV")
+        for g in range(0, 8):
             log(g)
-        for g in range(3 * CHUNK, GROUPS):
-            multiply_bb(x3, g, 0)
-            multiply_bb(x3, g, 1)
-
+        load_sigmoid_table()
+        for g in range(0, 8):
+            tanh(g)
+            times_z(g)
+        flip("r0", "VV")
+        quantise("rf")
+        after = ["r%d" % i for i in range(1, 8)] + ["x4"]
+        for i in range(8):
+            flip(after[i], "VV")
+            quantise("r%d" % i)
+            if i > 0:
+                multiply_rf(i - 1)
+        flip("x5", "VV")
+        quantise("x4")
+        multiply_rf(7)
+        sigmoid(RF)
+        quantise("x5")
+        for g in (8, 9):
+            multiply_bb(g, 0)
+            multiply_bb(g, 1)
+            sigmoid(g)
+        flip("x6", "VV")
+        for g in (10, 11):
+            multiply_bb(g, 0)
+            multiply_bb(g, 1)
+            sigmoid(g)
+        flip("x7", "VV")
+        quantise("x6")
+        log(RF)
+        for g in range(8, 12):
+            log(g)
         load_sigmoid_table()
         tanh(RF)
-        with_parked(RF, z_rf_banks, ALU.mult)
-        rf_banks = park(w[RF], flip_psum, "bank")
-        for g in range(0, 2 * CHUNK):
-            finish(g)
-        for g in range(3 * CHUNK, GROUPS):
+        for g in range(8, 12):
+            tanh(g)
+            times_z(g)
+        quantise("x7")
+        for g in range(12, 16):
+            multiply_bb(g, 0)
+            multiply_bb(g, 1)
             sigmoid(g)
-
-        for g in range(2 * CHUNK, 3 * CHUNK):
-            tanh(g)
-            times_z(nc.gpsimd, g)
-            finish(g)
-        for g in range(3 * CHUNK, GROUPS):
+        rf_banks = []
+        for h in range(D_BB // HALF):
+            cols = slice(h * HALF, (h + 1) * HALF)
+            nc.vector.tensor_tensor(out=w[RF][:, cols], in0=z[RF][:, cols], in1=w[RF][:, cols], op=ALU.mult)
+            rf_banks.append(park(w[RF], h, flip_psum, "bank"))
+        z_banks = {}
+        for g in (12, 14):
+            z_banks[g] = [park(z[g], h, acc_psum, "acc") for h in range(D_BB // HALF)]
+        for g in range(12, 16):
             log(g)
-        z_banks = [park(z[g], acc_psum, "acc") for g in range(3 * CHUNK + 1, GROUPS, 2)]
-        for g in range(3 * CHUNK, GROUPS, 2):
+        nc.gpsimd.tensor_tensor(out=w[7][:], in0=w[7][:], in1=w[RF][:], op=ALU.add)
+        for g in range(0, 12):
+            if g != 7:
+                finish(g)
+        store(7)
+        for g in (12, 14):
             tanh(g)
-            times_z(nc.gpsimd, g)
-            tanh(g + 1)
-            with_parked(g + 1, z_banks[(g - 3 * CHUNK) // 2], ALU.mult)
-            finish(g + 1)
+            with_parked(g, z_banks[g], ALU.mult)
             finish(g)
+            tanh(g + 1)
+            times_z(g + 1)
+            if g == 14:
+                finish(13)
+        for h, cols in enumerate((first, second)):
+            nc.vector.tensor_tensor(out=w[15][:, cols], in0=rf_banks[h][:], in1=w[15][:, cols], op=ALU.add)
+            store(15, cols)

@@ -18,6 +18,7 @@ D_RF = 2048
 HALF = 512
 PIECE = 2048
 WORDS = PIECE // 4
+BLOCKS = D_BB // P
 BLOCKS_PER_BANK = 4
 TINY = 2.0 ** -60
 
@@ -31,7 +32,7 @@ def tile_gnn_layer_pb_kernel(tc, BB_feature, RF_feature, W_bbbb, b_bbbb, W_rfbb,
         raw_pool = stack.enter_context(tc.tile_pool(name="raw", bufs=10))
         grouped_pool = stack.enter_context(tc.tile_pool(name="grouped", bufs=5))
         keep = stack.enter_context(tc.tile_pool(name="keep", bufs=1))
-        turn = stack.enter_context(tc.tile_pool(name="turn", bufs=6))
+        turn = stack.enter_context(tc.tile_pool(name="turn", bufs=4))
         work = stack.enter_context(tc.tile_pool(name="work", bufs=1))
         flip_psum = stack.enter_context(tc.psum_pool(name="flip", bufs=4))
         acc_psum = stack.enter_context(tc.psum_pool(name="acc", bufs=4))
@@ -43,7 +44,7 @@ def tile_gnn_layer_pb_kernel(tc, BB_feature, RF_feature, W_bbbb, b_bbbb, W_rfbb,
         for i in range(8):
             views["x%d" % i] = BB_feature[:, 2 * i : 2 * i + 2, :]
             views["r%d" % i] = W_rfbb[P * i : P * (i + 1), :].rearrange("(j p) k -> p j k", p=P)
-        to_load = ["w0", "x0", "w1", "x1", "w2", "w3", "x2", "x3", "rf"]
+        to_load = ["w0", "x0", "x1", "w1", "w2", "w3", "x2", "x3", "rf"]
         to_load += ["r%d" % i for i in range(8)] + ["x4", "x5", "x6", "x7"]
         raw = {}
         grouped = {}
@@ -57,12 +58,12 @@ def tile_gnn_layer_pb_kernel(tc, BB_feature, RF_feature, W_bbbb, b_bbbb, W_rfbb,
                 view = views[name]
                 nc.sync.dma_start(out=raw[name][:].rearrange("p (j k) -> p j k", j=view.shape[1]), in_=view)
 
-        bias_rows = const.tile([P, 2 * D_BB], BF16, name="bias_rows")
-        nc.vector.memset(bias_rows[:].bitcast(U32), 0)
+        bias_pad = const.tile([P, P], BF16, name="bias_pad")
+        nc.vector.memset(bias_pad[:].bitcast(U32), 0)
         for i in range(2):
             load()
-        nc.sync.dma_start(out=bias_rows[0:1, :D_BB], in_=b_bbbb.rearrange("(o n) -> o n", o=1))
-        nc.sync.dma_start(out=bias_rows[0:1, D_BB:], in_=b_rfbb.rearrange("(o n) -> o n", o=1))
+        nc.sync.dma_start(out=bias_pad[0:BLOCKS, :], in_=b_bbbb.rearrange("(c n) -> c n", n=P))
+        nc.sync.dma_start(out=bias_pad[BLOCKS : 2 * BLOCKS, :], in_=b_rfbb.rearrange("(c n) -> c n", n=P))
         for i in range(8):
             load()
 
@@ -71,8 +72,10 @@ def tile_gnn_layer_pb_kernel(tc, BB_feature, RF_feature, W_bbbb, b_bbbb, W_rfbb,
         tiny = const.tile([P, 1], F32, name="tiny")
         nc.vector.memset(tiny[:], TINY)
         warm = const.tile([P, 1], F32, name="warm")
-        ones = const.tile([P, P], BF16, name="ones")
-        nc.vector.memset(ones[:], 1.0)
+        picks = const.tile([P, 2 * BLOCKS], BF16, name="picks")
+        nc.vector.tensor_copy(out=picks[:], in_=ident[:, : 2 * BLOCKS])
+        bias_cols = const.tile([P, BLOCKS], F32, name="bias_cols")
+        minus_bias_cols = const.tile([P, BLOCKS], F32, name="minus_bias_cols")
         bias_bb = const.tile([P, D_BB], BF16, name="bias_bb")
         bias_rf = const.tile([P, D_BB], BF16, name="bias_rf")
 
@@ -81,12 +84,20 @@ def tile_gnn_layer_pb_kernel(tc, BB_feature, RF_feature, W_bbbb, b_bbbb, W_rfbb,
 
         load_sigmoid_table()
 
-        def spread_bias(spread, first):
+        def turn_bias():
+            acc = acc_psum.tile([P, HALF], F32, name="acc")
+            nc.tensor.matmul(out=acc[:, :BLOCKS], lhsT=bias_pad[:], rhs=picks[:, :BLOCKS], start=True, stop=True)
+            nc.vector.tensor_copy(out=bias_cols[:], in_=acc[:, :BLOCKS])
+            nc.vector.tensor_scalar(out=minus_bias_cols[:], in0=acc[:, :BLOCKS], scalar1=-1.0, scalar2=None, op0=ALU.mult)
+
+        def spread_bias(spread, first_row):
             for h in range(D_BB // HALF):
-                row = bias_rows[:, first + h * HALF : first + (h + 1) * HALF]
                 acc = acc_psum.tile([P, HALF], F32, name="acc")
-                nc.tensor.matmul(out=acc[:], lhsT=ones[:], rhs=row, start=True, stop=True)
-                nc.scalar.copy(out=spread[:, h * HALF : (h + 1) * HALF], in_=acc[:])
+                for i in range(HALF // P):
+                    r = first_row + h * (HALF // P) + i
+                    pick = picks[:, r : r + 1].to_broadcast([P, P])
+                    nc.tensor.matmul(out=acc[:, i * P : (i + 1) * P], lhsT=pick, rhs=bias_pad[:], start=True, stop=True)
+                nc.vector.tensor_copy(out=spread[:, h * HALF : (h + 1) * HALF], in_=acc[:])
 
         z = [work.tile([P, D_BB], F32, name="z%d" % g) for g in range(GROUPS + 1)]
         w = [work.tile([P, D_BB], F32, name="w%d" % g) for g in range(GROUPS + 1)]
@@ -115,8 +126,9 @@ def tile_gnn_layer_pb_kernel(tc, BB_feature, RF_feature, W_bbbb, b_bbbb, W_rfbb,
             load()
 
         def quantise(name):
-            pool = turn if name[0] == "x" or (name[0] == "r" and name != "rf") else keep
-            tag = "turn" if pool is turn else name
+            passing = name in ("x4", "x5", "x6", "x7") or (name[0] == "r" and name != "rf")
+            pool = turn if passing else keep
+            tag = "turn" if passing else name
             codes = pool.tile([P, WORDS], U32, name="codes_" + tag, align_bytes=64)
             scales = pool.tile([P, WORDS], U8, name="scales_" + tag, align_bytes=64)
             nc.vector.quantize_mx(out=codes[:].bitcast(FP8X4), scales=scales[:], in_=grouped[name][:])
@@ -144,6 +156,40 @@ def tile_gnn_layer_pb_kernel(tc, BB_feature, RF_feature, W_bbbb, b_bbbb, W_rfbb,
                 product(acc[:, 2 * P * i : 2 * P * (i + 1)], "x%d" % (g // 2), g % 2, 2, "w%d" % (2 * h + i), 2 * P, 2)
             cols = slice(h * HALF, (h + 1) * HALF)
             nc.vector.tensor_tensor(out=z[g][:, cols], in0=acc[:], in1=bias_bb[:, cols], op=ALU.add)
+
+        def turned(q, n):
+            return w[4 * q + n // 2][:, n % 2 * HALF : (n % 2 + 1) * HALF]
+
+        def multiply_turned(q, n):
+            acc = acc_psum.tile([P, HALF], F32, name="acc")
+            for i in range(2):
+                product(acc[:, 2 * P * i : 2 * P * (i + 1)], "w%d" % (n // 2), n % 2, 2, "x%d" % (2 * q + i), 2 * P, 2)
+            return acc
+
+        def sigmoid_turned(q, n):
+            acc = multiply_turned(q, n)
+            nc.scalar.activation(
+                out=turned(q, n), in_=acc[:], func=FUNC.Sigmoid, scale=-1.0, bias=minus_bias_cols[:, n : n + 1]
+            )
+
+        def times_z_turned(q, n):
+            acc = multiply_turned(q, n)
+            nc.vector.scalar_tensor_tensor(
+                out=turned(q, n), in0=acc[:], scalar=bias_cols[:, n : n + 1], in1=turned(q, n), op0=ALU.add, op1=ALU.mult
+            )
+
+        def finish_turned(g):
+            for h in range(D_BB // HALF):
+                if g % 2 == 0:
+                    bank = acc_psum.tile([P, HALF], F32, name="acc")
+                else:
+                    bank = flip_psum.tile([P, HALF], F32, name="bank")
+                for i in range(BLOCKS_PER_BANK):
+                    block = turned(g // 4, BLOCKS_PER_BANK * h + i)[:, g % 4 * P : (g % 4 + 1) * P]
+                    nc.tensor.transpose(bank[:, i * P : (i + 1) * P], block, ident[:])
+                cols = slice(h * HALF, (h + 1) * HALF)
+                nc.vector.tensor_tensor(out=z[g][:, cols], in0=bank[:], in1=w[RF][:, cols], op=ALU.add)
+            nc.sync.dma_start(out=out[:, g, :], in_=z[g][:])
 
         rf_acc = []
 
@@ -189,51 +235,33 @@ def tile_gnn_layer_pb_kernel(tc, BB_feature, RF_feature, W_bbbb, b_bbbb, W_rfbb,
         first = slice(0, HALF)
         second = slice(HALF, D_BB)
 
-        flip("w0", "VS")
-        flip("x0", "VS")
-        quantise("w0")
-        quantise("x0")
-        flip("w1", "SS")
-        quantise("w1")
-        spread_bias(bias_bb, 0)
-        flip("x1", "VS")
-        for g in (0, 1):
-            multiply_bb(g, 0)
-        for g in (0, 1):
-            sigmoid(g, first)
-        quantise("x1")
-        flip("w2", "VS")
-        flip("w3", "VS")
-        for g in (2, 3):
-            multiply_bb(g, 0)
-        for g in (2, 3):
-            sigmoid(g, first)
-        quantise("w2")
-        quantise("w3")
-        flip("x2", "SS")
-        flip("x3", "SV")
-        for g in (0, 1):
-            multiply_bb(g, 1)
-            sigmoid(g, second)
-        quantise("x2")
-        spread_bias(bias_rf, D_BB)
-        for g in (2, 3):
-            multiply_bb(g, 1)
-            sigmoid(g, second)
+        head = ["w0", "x0", "x1", "w1", "w2", "w3", "x2", "x3"]
+        for i, name in enumerate(head):
+            flip(name, "SS" if name == "w1" else "VS")
+            if name == "x1":
+                turn_bias()
+            if i > 0:
+                quantise(head[i - 1])
+            if i > 3:
+                sigmoid_turned(0, i - 4)
         quantise("x3")
-        for g in range(4, 8):
-            multiply_bb(g, 0)
-            multiply_bb(g, 1)
-            sigmoid(g)
+        for n in range(4, 8):
+            sigmoid_turned(0, n)
         flip("rf", "VV")
+        for n in range(0, 4):
+            sigmoid_turned(1, n)
+        flip("r0", "VV")
+        quantise("rf")
+        for n in range(4, 8):
+            sigmoid_turned(1, n)
+        spread_bias(bias_rf, BLOCKS)
+        spread_bias(bias_bb, 0)
         for g in range(0, 8):
             log(g)
         load_sigmoid_table()
         for g in range(0, 8):
             tanh(g)
-            times_z(g)
-        flip("r0", "VV")
-        quantise("rf")
+
         after = ["r%d" % i for i in range(1, 8)] + ["x4"]
         for i in range(8):
             flip(after[i], "VV")
@@ -259,31 +287,42 @@ def tile_gnn_layer_pb_kernel(tc, BB_feature, RF_feature, W_bbbb, b_bbbb, W_rfbb,
         log(RF)
         for g in range(8, 12):
             log(g)
+        quantise("x7")
         load_sigmoid_table()
         tanh(RF)
         for g in range(8, 12):
             tanh(g)
             times_z(g)
-        quantise("x7")
-        for g in range(12, 16):
+        for q in range(2):
+            for n in range(BLOCKS):
+                times_z_turned(q, n)
+
+        def open_last(g):
             multiply_bb(g, 0)
             multiply_bb(g, 1)
             sigmoid(g)
-        rf_banks = []
-        for h in range(D_BB // HALF):
-            cols = slice(h * HALF, (h + 1) * HALF)
+
+        open_last(12)
+        for cols in (first, second):
             nc.vector.tensor_tensor(out=w[RF][:, cols], in0=z[RF][:, cols], in1=w[RF][:, cols], op=ALU.mult)
-            rf_banks.append(park(w[RF], h, flip_psum, "bank"))
+        open_last(13)
+        finish_turned(0)
+        open_last(14)
+        finish_turned(1)
+        open_last(15)
+        for g in range(12, 16):
+            log(g)
+        for g in range(8, 11):
+            nc.gpsimd.tensor_tensor(out=w[g][:], in0=w[g][:], in1=w[RF][:], op=ALU.add)
+        for g in range(2, 8):
+            finish_turned(g)
+            if g > 4:
+                store(g + 3)
+        rf_banks = [park(w[RF], h, flip_psum, "bank") for h in range(D_BB // HALF)]
         z_banks = {}
         for g in (12, 14):
             z_banks[g] = [park(z[g], h, acc_psum, "acc") for h in range(D_BB // HALF)]
-        for g in range(12, 16):
-            log(g)
-        nc.gpsimd.tensor_tensor(out=w[7][:], in0=w[7][:], in1=w[RF][:], op=ALU.add)
-        for g in range(0, 12):
-            if g != 7:
-                finish(g)
-        store(7)
+        finish(11)
         for g in (12, 14):
             tanh(g)
             with_parked(g, z_banks[g], ALU.mult)

@@ -50,6 +50,9 @@ def tile_gnn_layer_pb_kernel(tc, BB_feature, RF_feature, W_bbbb, b_bbbb, W_rfbb,
         grouped = {}
         mx = {}
 
+        bias_bb = const.tile([P, D_BB], BF16, name="bias_bb")
+        bias_rf = const.tile([P, D_BB], BF16, name="bias_rf")
+
         def load():
             if to_load:
                 name = to_load[0]
@@ -57,13 +60,15 @@ def tile_gnn_layer_pb_kernel(tc, BB_feature, RF_feature, W_bbbb, b_bbbb, W_rfbb,
                 raw[name] = raw_pool.tile([P, PIECE], BF16, name="raw")
                 view = views[name]
                 nc.sync.dma_start(out=raw[name][:].rearrange("p (j k) -> p j k", j=view.shape[1]), in_=view)
+                if name == "r7":
+                    nc.sync.dma_start(out=bias_rf[:], in_=b_rfbb.partition_broadcast(P))
+                    nc.sync.dma_start(out=bias_bb[:], in_=b_bbbb.partition_broadcast(P))
 
         bias_pad = const.tile([P, P], BF16, name="bias_pad")
         nc.vector.memset(bias_pad[:].bitcast(U32), 0)
         for i in range(2):
             load()
         nc.sync.dma_start(out=bias_pad[0:BLOCKS, :], in_=b_bbbb.rearrange("(c n) -> c n", n=P))
-        nc.sync.dma_start(out=bias_pad[BLOCKS : 2 * BLOCKS, :], in_=b_rfbb.rearrange("(c n) -> c n", n=P))
         for i in range(8):
             load()
 
@@ -72,12 +77,10 @@ def tile_gnn_layer_pb_kernel(tc, BB_feature, RF_feature, W_bbbb, b_bbbb, W_rfbb,
         tiny = const.tile([P, 1], F32, name="tiny")
         nc.vector.memset(tiny[:], TINY)
         warm = const.tile([P, 1], F32, name="warm")
-        picks = const.tile([P, 2 * BLOCKS], BF16, name="picks")
-        nc.vector.tensor_copy(out=picks[:], in_=ident[:, : 2 * BLOCKS])
+        picks = const.tile([P, BLOCKS], BF16, name="picks")
+        nc.vector.tensor_copy(out=picks[:], in_=ident[:, :BLOCKS])
         bias_cols = const.tile([P, BLOCKS], F32, name="bias_cols")
         minus_bias_cols = const.tile([P, BLOCKS], F32, name="minus_bias_cols")
-        bias_bb = const.tile([P, D_BB], BF16, name="bias_bb")
-        bias_rf = const.tile([P, D_BB], BF16, name="bias_rf")
 
         def load_sigmoid_table():
             nc.scalar.activation(out=warm[:], in_=tiny[:], func=FUNC.Sigmoid)
@@ -86,18 +89,9 @@ def tile_gnn_layer_pb_kernel(tc, BB_feature, RF_feature, W_bbbb, b_bbbb, W_rfbb,
 
         def turn_bias():
             acc = acc_psum.tile([P, HALF], F32, name="acc")
-            nc.tensor.matmul(out=acc[:, :BLOCKS], lhsT=bias_pad[:], rhs=picks[:, :BLOCKS], start=True, stop=True)
+            nc.tensor.matmul(out=acc[:, :BLOCKS], lhsT=bias_pad[:], rhs=picks[:], start=True, stop=True)
             nc.vector.tensor_copy(out=bias_cols[:], in_=acc[:, :BLOCKS])
             nc.vector.tensor_scalar(out=minus_bias_cols[:], in0=acc[:, :BLOCKS], scalar1=-1.0, scalar2=None, op0=ALU.mult)
-
-        def spread_bias(spread, first_row):
-            for h in range(D_BB // HALF):
-                acc = acc_psum.tile([P, HALF], F32, name="acc")
-                for i in range(HALF // P):
-                    r = first_row + h * (HALF // P) + i
-                    pick = picks[:, r : r + 1].to_broadcast([P, P])
-                    nc.tensor.matmul(out=acc[:, i * P : (i + 1) * P], lhsT=pick, rhs=bias_pad[:], start=True, stop=True)
-                nc.vector.tensor_copy(out=spread[:, h * HALF : (h + 1) * HALF], in_=acc[:])
 
         z = [work.tile([P, D_BB], F32, name="z%d" % g) for g in range(GROUPS + 1)]
         w = [work.tile([P, D_BB], F32, name="w%d" % g) for g in range(GROUPS + 1)]
@@ -254,8 +248,6 @@ def tile_gnn_layer_pb_kernel(tc, BB_feature, RF_feature, W_bbbb, b_bbbb, W_rfbb,
         quantise("rf")
         for n in range(4, 8):
             sigmoid_turned(1, n)
-        spread_bias(bias_rf, BLOCKS)
-        spread_bias(bias_bb, 0)
         for g in range(0, 8):
             log(g)
         load_sigmoid_table()

@@ -59,7 +59,12 @@ def tile_gnn_layer_pb_kernel(tc, BB_feature, RF_feature, W_bbbb, b_bbbb, W_rfbb,
                 to_load.remove(name)
                 raw[name] = raw_pool.tile([P, PIECE], BF16, name="raw")
                 view = views[name]
-                nc.sync.dma_start(out=raw[name][:].rearrange("p (j k) -> p j k", j=view.shape[1]), in_=view)
+                dst = raw[name][:].rearrange("p (j k) -> p j k", j=view.shape[1])
+                if name in ("w0", "x0"):
+                    for j in range(2):
+                        nc.sync.dma_start(out=dst[:, j], in_=view[:, j])
+                else:
+                    nc.sync.dma_start(out=dst, in_=view)
                 if name == "r7":
                     nc.sync.dma_start(out=bias_rf[:], in_=b_rfbb.partition_broadcast(P))
                     nc.sync.dma_start(out=bias_bb[:], in_=b_bbbb.partition_broadcast(P))
@@ -72,6 +77,15 @@ def tile_gnn_layer_pb_kernel(tc, BB_feature, RF_feature, W_bbbb, b_bbbb, W_rfbb,
         for i in range(8):
             load()
 
+        zeros = const.tile([P, HALF], BF16, name="zeros")
+        nc.vector.memset(zeros[:].bitcast(U32), 0)
+        idle = acc_psum.tile([P, HALF], F32, name="acc")
+
+        def keep_clock_up(products):
+            for i in range(products):
+                nc.tensor.matmul(out=idle[:], lhsT=zeros[:, :P], rhs=zeros[:], start=True, stop=True)
+
+        keep_clock_up(6)
         ident = const.tile([P, P], F32, name="ident")
         make_identity(nc, ident[:])
         tiny = const.tile([P, 1], F32, name="tiny")
@@ -232,6 +246,8 @@ def tile_gnn_layer_pb_kernel(tc, BB_feature, RF_feature, W_bbbb, b_bbbb, W_rfbb,
         head = ["w0", "x0", "x1", "w1", "w2", "w3", "x2", "x3"]
         for i, name in enumerate(head):
             flip(name, "SS" if name == "w1" else "VS")
+            if i < 4:
+                keep_clock_up(1)
             if name == "x1":
                 turn_bias()
             if i > 0:

@@ -85,7 +85,7 @@ def tile_gnn_layer_pb_kernel(tc, BB_feature, RF_feature, W_bbbb, b_bbbb, W_rfbb,
             for i in range(products):
                 nc.tensor.matmul(out=idle[:], lhsT=zeros[:, :P], rhs=zeros[:], start=True, stop=True)
 
-        keep_clock_up(6)
+        keep_clock_up(5)
         ident = const.tile([P, P], F32, name="ident")
         make_identity(nc, ident[:])
         tiny = const.tile([P, 1], F32, name="tiny")
@@ -108,7 +108,8 @@ def tile_gnn_layer_pb_kernel(tc, BB_feature, RF_feature, W_bbbb, b_bbbb, W_rfbb,
             nc.vector.tensor_scalar(out=minus_bias_cols[:], in0=acc[:, :BLOCKS], scalar1=-1.0, scalar2=None, op0=ALU.mult)
 
         z = [work.tile([P, D_BB], F32, name="z%d" % g) for g in range(GROUPS + 1)]
-        w = [work.tile([P, D_BB], F32, name="w%d" % g) for g in range(GROUPS + 1)]
+        w_all = work.tile([P, (GROUPS + 1) * D_BB], F32, name="w_all")
+        w = [w_all[:, g * D_BB : (g + 1) * D_BB] for g in range(GROUPS + 1)]
         RF = GROUPS
 
         def flip(name, copies):
@@ -214,14 +215,16 @@ def tile_gnn_layer_pb_kernel(tc, BB_feature, RF_feature, W_bbbb, b_bbbb, W_rfbb,
         def sigmoid(g, cols=slice(0, D_BB)):
             nc.scalar.activation(out=w[g][:, cols], in_=z[g][:, cols], func=FUNC.Sigmoid, scale=-1.0)
 
-        def log(g):
-            nc.scalar.activation(out=w[g][:], in_=w[g][:], func=FUNC.Ln, bias=tiny[:])
+        def log(g, groups=1):
+            part = w_all[:, g * D_BB : (g + groups) * D_BB]
+            nc.scalar.activation(out=part, in_=part, func=FUNC.Ln, bias=tiny[:])
 
-        def tanh(g):
-            nc.scalar.activation(out=w[g][:], in_=w[g][:], func=FUNC.Tanh, scale=-1.0)
+        def tanh(g, groups=1):
+            part = w_all[:, g * D_BB : (g + groups) * D_BB]
+            nc.scalar.activation(out=part, in_=part, func=FUNC.Tanh, scale=-1.0)
 
         def times_z(g):
-            nc.gpsimd.tensor_tensor(out=w[g][:], in0=z[g][:], in1=w[g][:], op=ALU.mult)
+            nc.gpsimd.tensor_tensor(out=w[g], in0=z[g][:], in1=w[g], op=ALU.mult)
 
         def park(values, h, pool, name):
             bank = pool.tile([P, HALF], F32, name=name)
@@ -244,31 +247,29 @@ def tile_gnn_layer_pb_kernel(tc, BB_feature, RF_feature, W_bbbb, b_bbbb, W_rfbb,
         second = slice(HALF, D_BB)
 
         head = ["w0", "x0", "x1", "w1", "w2", "w3", "x2", "x3"]
+        units = [(q, n) for q in range(2) for n in range(BLOCKS)]
+        behind = {"w1": 1, "w3": 2, "x3": 13}
         for i, name in enumerate(head):
             flip(name, "SS" if name == "w1" else "VS")
-            if i < 4:
+            if name == "x0":
                 keep_clock_up(1)
             if name == "x1":
                 turn_bias()
             if i > 0:
                 quantise(head[i - 1])
-            if i > 3:
-                sigmoid_turned(0, i - 4)
-        quantise("x3")
-        for n in range(4, 8):
-            sigmoid_turned(0, n)
-        flip("rf", "VV")
-        for n in range(0, 4):
-            sigmoid_turned(1, n)
+            if name == "x3":
+                quantise("x3")
+            for k in range(behind.get(name, 0)):
+                sigmoid_turned(units[0][0], units[0][1])
+                units.remove(units[0])
+        flip("rf", "VS")
         flip("r0", "VV")
         quantise("rf")
-        for n in range(4, 8):
-            sigmoid_turned(1, n)
-        for g in range(0, 8):
-            log(g)
+        for q in range(2):
+            log(4 * q, 4)
         load_sigmoid_table()
-        for g in range(0, 8):
-            tanh(g)
+        for q in range(2):
+            tanh(4 * q, 4)
 
         after = ["r%d" % i for i in range(1, 8)] + ["x4"]
         for i in range(8):
@@ -293,8 +294,7 @@ def tile_gnn_layer_pb_kernel(tc, BB_feature, RF_feature, W_bbbb, b_bbbb, W_rfbb,
         flip("x7", "VV")
         quantise("x6")
         log(RF)
-        for g in range(8, 12):
-            log(g)
+        log(8, 4)
         quantise("x7")
         load_sigmoid_table()
         tanh(RF)
@@ -318,10 +318,9 @@ def tile_gnn_layer_pb_kernel(tc, BB_feature, RF_feature, W_bbbb, b_bbbb, W_rfbb,
         open_last(14)
         finish_turned(1)
         open_last(15)
-        for g in range(12, 16):
-            log(g)
+        log(12, 4)
         for g in range(8, 11):
-            nc.gpsimd.tensor_tensor(out=w[g][:], in0=w[g][:], in1=w[RF][:], op=ALU.add)
+            nc.gpsimd.tensor_tensor(out=w[g], in0=w[g], in1=w[RF], op=ALU.add)
         for g in range(2, 8):
             finish_turned(g)
             if g > 4:

@@ -262,7 +262,7 @@ def tile_gnn_layer_pb_kernel(tc, BB_feature, RF_feature, W_bbbb, b_bbbb, W_rfbb,
             for k in range(behind.get(name, 0)):
                 sigmoid_turned(units[0][0], units[0][1])
                 units.remove(units[0])
-        flip("rf", "VS")
+        flip("rf", "VV")
         flip("r0", "VV")
         quantise("rf")
         for q in range(2):
@@ -282,15 +282,11 @@ def tile_gnn_layer_pb_kernel(tc, BB_feature, RF_feature, W_bbbb, b_bbbb, W_rfbb,
         multiply_rf(7)
         sigmoid(RF)
         quantise("x5")
-        for g in (8, 9):
+        for g in range(8, 12):
             multiply_bb(g, 0)
             multiply_bb(g, 1)
             sigmoid(g)
         flip("x6", "VV")
-        for g in (10, 11):
-            multiply_bb(g, 0)
-            multiply_bb(g, 1)
-            sigmoid(g)
         flip("x7", "VV")
         quantise("x6")
         log(RF)

@@ -294,37 +294,32 @@ def tile_gnn_layer_pb_kernel(tc, BB_feature, RF_feature, W_bbbb, b_bbbb, W_rfbb,
         quantise("x7")
         load_sigmoid_table()
         tanh(RF)
+        times_z(RF)
         for g in range(8, 12):
             tanh(g)
             times_z(g)
-        for q in range(2):
-            for n in range(BLOCKS):
-                times_z_turned(q, n)
-
-        def open_last(g):
+        for g in range(12, 16):
             multiply_bb(g, 0)
             multiply_bb(g, 1)
             sigmoid(g)
-
-        open_last(12)
-        for cols in (first, second):
-            nc.vector.tensor_tensor(out=w[RF][:, cols], in0=z[RF][:, cols], in1=w[RF][:, cols], op=ALU.mult)
-        open_last(13)
-        finish_turned(0)
-        open_last(14)
-        finish_turned(1)
-        open_last(15)
-        log(12, 4)
-        for g in range(8, 11):
-            nc.gpsimd.tensor_tensor(out=w[g], in0=w[g], in1=w[RF], op=ALU.add)
-        for g in range(2, 8):
+        for n in range(BLOCKS):
+            times_z_turned(0, n)
+        for g in range(0, 4):
             finish_turned(g)
-            if g > 4:
-                store(g + 3)
+        log(12, 4)
+        for g in (8, 9):
+            nc.gpsimd.tensor_tensor(out=w[g], in0=w[g], in1=w[RF], op=ALU.add)
+        for n in range(BLOCKS):
+            times_z_turned(1, n)
+        for g in range(4, 8):
+            finish_turned(g)
+            if g > 5:
+                store(g + 2)
         rf_banks = [park(w[RF], h, flip_psum, "bank") for h in range(D_BB // HALF)]
         z_banks = {}
         for g in (12, 14):
             z_banks[g] = [park(z[g], h, acc_psum, "acc") for h in range(D_BB // HALF)]
+        finish(10)
         finish(11)
         for g in (12, 14):
             tanh(g)

@@ -91,6 +91,7 @@ def tile_gnn_layer_pb_kernel(tc, BB_feature, RF_feature, W_bbbb, b_bbbb, W_rfbb,
         tiny = const.tile([P, 1], F32, name="tiny")
         nc.vector.memset(tiny[:], TINY)
         warm = const.tile([P, 1], F32, name="warm")
+        gate = const.tile([P, 1], F32, name="gate")
         picks = const.tile([P, BLOCKS], BF16, name="picks")
         nc.vector.tensor_copy(out=picks[:], in_=ident[:, :BLOCKS])
         bias_cols = const.tile([P, BLOCKS], F32, name="bias_cols")
@@ -107,7 +108,8 @@ def tile_gnn_layer_pb_kernel(tc, BB_feature, RF_feature, W_bbbb, b_bbbb, W_rfbb,
             nc.vector.tensor_copy(out=bias_cols[:], in_=acc[:, :BLOCKS])
             nc.vector.tensor_scalar(out=minus_bias_cols[:], in0=acc[:, :BLOCKS], scalar1=-1.0, scalar2=None, op0=ALU.mult)
 
-        z = [work.tile([P, D_BB], F32, name="z%d" % g) for g in range(GROUPS + 1)]
+        z_tiles = [work.tile([P, D_BB], F32, name="z%d" % g) for g in range(GROUPS + 1)]
+        z = [tile[:] for tile in z_tiles]
         w_all = work.tile([P, (GROUPS + 1) * D_BB], F32, name="w_all")
         w = [w_all[:, g * D_BB : (g + 1) * D_BB] for g in range(GROUPS + 1)]
         RF = GROUPS
@@ -198,7 +200,7 @@ def tile_gnn_layer_pb_kernel(tc, BB_feature, RF_feature, W_bbbb, b_bbbb, W_rfbb,
                     nc.tensor.transpose(bank[:, i * P : (i + 1) * P], block, ident[:])
                 cols = slice(h * HALF, (h + 1) * HALF)
                 nc.vector.tensor_tensor(out=z[g][:, cols], in0=bank[:], in1=w[RF][:, cols], op=ALU.add)
-            nc.sync.dma_start(out=out[:, g, :], in_=z[g][:])
+            nc.sync.dma_start(out=out[:, g, :], in_=z[g])
 
         rf_acc = []
 
@@ -224,7 +226,7 @@ def tile_gnn_layer_pb_kernel(tc, BB_feature, RF_feature, W_bbbb, b_bbbb, W_rfbb,
             nc.scalar.activation(out=part, in_=part, func=FUNC.Tanh, scale=-1.0)
 
         def times_z(g):
-            nc.gpsimd.tensor_tensor(out=w[g], in0=z[g][:], in1=w[g], op=ALU.mult)
+            nc.gpsimd.tensor_tensor(out=w[g], in0=z[g], in1=w[g], op=ALU.mult)
 
         def park(values, h, pool, name):
             bank = pool.tile([P, HALF], F32, name=name)
@@ -294,23 +296,24 @@ def tile_gnn_layer_pb_kernel(tc, BB_feature, RF_feature, W_bbbb, b_bbbb, W_rfbb,
         quantise("x7")
         load_sigmoid_table()
         tanh(RF)
-        times_z(RF)
         for g in range(8, 12):
             tanh(g)
+        for q in range(2):
+            for n in range(BLOCKS):
+                times_z_turned(q, n)
+        nc.vector.tensor_tensor(out=w[RF], in0=z[RF], in1=w[RF], op=ALU.mult)
+        nc.gpsimd.tensor_copy(out=gate[:], in_=w[RF][:, :1])
+        for g in range(8, 12):
             times_z(g)
         for g in range(12, 16):
             multiply_bb(g, 0)
             multiply_bb(g, 1)
             sigmoid(g)
-        for n in range(BLOCKS):
-            times_z_turned(0, n)
         for g in range(0, 4):
             finish_turned(g)
         log(12, 4)
         for g in (8, 9):
             nc.gpsimd.tensor_tensor(out=w[g], in0=w[g], in1=w[RF], op=ALU.add)
-        for n in range(BLOCKS):
-            times_z_turned(1, n)
         for g in range(4, 8):
             finish_turned(g)
             if g > 5:

@@ -30,9 +30,9 @@ def tile_gnn_layer_pb_kernel(tc, BB_feature, RF_feature, W_bbbb, b_bbbb, W_rfbb,
     with ExitStack() as stack:
         const = stack.enter_context(tc.tile_pool(name="const", bufs=1))
         raw_pool = stack.enter_context(tc.tile_pool(name="raw", bufs=10))
-        grouped_pool = stack.enter_context(tc.tile_pool(name="grouped", bufs=5))
+        grouped_pool = stack.enter_context(tc.tile_pool(name="grouped", bufs=4))
         keep = stack.enter_context(tc.tile_pool(name="keep", bufs=1))
-        turn = stack.enter_context(tc.tile_pool(name="turn", bufs=4))
+        turn = stack.enter_context(tc.tile_pool(name="turn", bufs=6))
         work = stack.enter_context(tc.tile_pool(name="work", bufs=1))
         flip_psum = stack.enter_context(tc.psum_pool(name="flip", bufs=4))
         acc_psum = stack.enter_context(tc.psum_pool(name="acc", bufs=4))
@@ -277,11 +277,13 @@ def tile_gnn_layer_pb_kernel(tc, BB_feature, RF_feature, W_bbbb, b_bbbb, W_rfbb,
         for i in range(8):
             flip(after[i], "VV")
             quantise("r%d" % i)
-            if i > 0:
-                multiply_rf(i - 1)
+            if i == 4:
+                for k in range(0, 4):
+                    multiply_rf(k)
         flip("x5", "VV")
         quantise("x4")
-        multiply_rf(7)
+        for k in range(4, 8):
+            multiply_rf(k)
         sigmoid(RF)
         quantise("x5")
         for g in range(8, 12):

from contextlib import ExitStack

import concourse.mybir as mybir
from concourse.masks import make_identity

F32 = mybir.dt.float32
BF16 = mybir.dt.bfloat16
U32 = mybir.dt.uint32
U8 = mybir.dt.uint8
FP8X4 = mybir.dt.float8_e4m3fn_x4
FUNC = mybir.ActivationFunctionType
ALU = mybir.AluOpType

P = 128
GROUPS = 16
D_BB = 1024
D_RF = 2048
HALF = 512
PIECE = 2048
WORDS = PIECE // 4
BLOCKS = D_BB // P
BLOCKS_PER_BANK = 4
TINY = 2.0 ** -60

FLOPS = 2 * P * GROUPS * D_BB * D_BB + 2 * P * D_RF * D_BB


def tile_gnn_layer_pb_kernel(tc, BB_feature, RF_feature, W_bbbb, b_bbbb, W_rfbb, b_rfbb, out):
    nc = tc.nc
    with ExitStack() as stack:
        const = stack.enter_context(tc.tile_pool(name="const", bufs=1))
        raw_pool = stack.enter_context(tc.tile_pool(name="raw", bufs=10))
        grouped_pool = stack.enter_context(tc.tile_pool(name="grouped", bufs=4))
        keep = stack.enter_context(tc.tile_pool(name="keep", bufs=1))
        turn = stack.enter_context(tc.tile_pool(name="turn", bufs=6))
        work = stack.enter_context(tc.tile_pool(name="work", bufs=1))
        flip_psum = stack.enter_context(tc.psum_pool(name="flip", bufs=4))
        acc_psum = stack.enter_context(tc.psum_pool(name="acc", bufs=4))
        stack.enter_context(tc.manual_schedule())

        views = {"rf": RF_feature.rearrange("b (j k) -> b j k", j=1)}
        for i in range(4):
            views["w%d" % i] = W_bbbb[2 * P * i : 2 * P * (i + 1), :].rearrange("(j p) k -> p j k", p=P)
        for i in range(8):
            views["x%d" % i] = BB_feature[:, 2 * i : 2 * i + 2, :]
            views["r%d" % i] = W_rfbb[P * i : P * (i + 1), :].rearrange("(j p) k -> p j k", p=P)
        to_load = ["w0", "x0", "x1", "w1", "w2", "w3", "x2", "x3", "rf"]
        to_load += ["r%d" % i for i in range(8)] + ["x4", "x5", "x6", "x7"]
        raw = {}
        grouped = {}
        mx = {}

        bias_bb = const.tile([P, D_BB], BF16, name="bias_bb")
        bias_rf = const.tile([P, D_BB], BF16, name="bias_rf")

        def load():
            if to_load:
                name = to_load[0]
                to_load.remove(name)
                raw[name] = raw_pool.tile([P, PIECE], BF16, name="raw")
                view = views[name]
                dst = raw[name][:].rearrange("p (j k) -> p j k", j=view.shape[1])
                if name in ("w0", "x0"):
                    for j in range(2):
                        nc.sync.dma_start(out=dst[:, j], in_=view[:, j])
                else:
                    nc.sync.dma_start(out=dst, in_=view)
                if name == "r7":
                    nc.sync.dma_start(out=bias_rf[:], in_=b_rfbb.partition_broadcast(P))
                    nc.sync.dma_start(out=bias_bb[:], in_=b_bbbb.partition_broadcast(P))

        bias_pad = const.tile([P, P], BF16, name="bias_pad")
        nc.vector.memset(bias_pad[:].bitcast(U32), 0)
        for i in range(2):
            load()
        nc.sync.dma_start(out=bias_pad[0:BLOCKS, :], in_=b_bbbb.rearrange("(c n) -> c n", n=P))
        for i in range(8):
            load()

        zeros = const.tile([P, HALF], BF16, name="zeros")
        nc.vector.memset(zeros[:].bitcast(U32), 0)
        idle = acc_psum.tile([P, HALF], F32, name="acc")

        def keep_clock_up(products):
            for i in range(products):
                nc.tensor.matmul(out=idle[:], lhsT=zeros[:, :P], rhs=zeros[:], start=True, stop=True)

        keep_clock_up(5)
        ident = const.tile([P, P], F32, name="ident")
        make_identity(nc, ident[:])
        tiny = const.tile([P, 1], F32, name="tiny")
        nc.vector.memset(tiny[:], TINY)
        warm = const.tile([P, 1], F32, name="warm")
        gate = const.tile([P, 1], F32, name="gate")
        picks = const.tile([P, BLOCKS], BF16, name="picks")
        nc.vector.tensor_copy(out=picks[:], in_=ident[:, :BLOCKS])
        bias_cols = const.tile([P, BLOCKS], F32, name="bias_cols")
        minus_bias_cols = const.tile([P, BLOCKS], F32, name="minus_bias_cols")

        def load_sigmoid_table():
            nc.scalar.activation(out=warm[:], in_=tiny[:], func=FUNC.Sigmoid)

        load_sigmoid_table()

        def turn_bias():
            acc = acc_psum.tile([P, HALF], F32, name="acc")
            nc.tensor.matmul(out=acc[:, :BLOCKS], lhsT=bias_pad[:], rhs=picks[:], start=True, stop=True)
            nc.vector.tensor_copy(out=bias_cols[:], in_=acc[:, :BLOCKS])
            nc.vector.tensor_scalar(out=minus_bias_cols[:], in0=acc[:, :BLOCKS], scalar1=-1.0, scalar2=None, op0=ALU.mult)

        z_tiles = [work.tile([P, D_BB], F32, name="z%d" % g) for g in range(GROUPS + 1)]
        z = [tile[:] for tile in z_tiles]
        w_all = work.tile([P, (GROUPS + 1) * D_BB], F32, name="w_all")
        w = [w_all[:, g * D_BB : (g + 1) * D_BB] for g in range(GROUPS + 1)]
        RF = GROUPS

        def flip(name, copies):
            words = raw[name][:].bitcast(F32)
            row_tiles = views[name].shape[1]
            passes = 4 // row_tiles
            grouped[name] = grouped_pool.tile([P, PIECE], BF16, name="grouped", align_bytes=64)
            pairs = grouped[name][:].bitcast(F32).rearrange(
                "p (c j r u) -> p c j r u", c=passes, j=row_tiles, u=2
            )
            for b in range(2):
                bank = flip_psum.tile([P, BLOCKS_PER_BANK, P], F32, name="bank")
                for s in range(BLOCKS_PER_BANK):
                    n = BLOCKS_PER_BANK * b + s
                    pair = n // 2 * 2 * P
                    nc.tensor.transpose(bank[:, s, :], words[:, pair + n % 2 : pair + 2 * P : 2], ident[:])
                dst = pairs[:, 0:2, b] if row_tiles == 2 else pairs[:, 2 * b : 2 * b + 2, 0]
                src = bank[:].rearrange("p (c u) r -> p c r u", u=2)
                if copies[b] == "S":
                    nc.scalar.copy(out=dst, in_=src)
                else:
                    nc.vector.tensor_copy(out=dst, in_=src)
            load()

        def quantise(name):
            passing = name in ("x4", "x5", "x6", "x7") or (name[0] == "r" and name != "rf")
            pool = turn if passing else keep
            tag = "turn" if passing else name
            codes = pool.tile([P, WORDS], U32, name="codes_" + tag, align_bytes=64)
            scales = pool.tile([P, WORDS], U8, name="scales_" + tag, align_bytes=64)
            nc.vector.quantize_mx(out=codes[:].bitcast(FP8X4), scales=scales[:], in_=grouped[name][:])
            mx[name] = (codes, scales)

        def product(acc, stationary, j, row_tiles, moving, width, passes):
            s_codes, s_scales = mx[stationary]
            m_codes, m_scales = mx[moving]
            for c in range(passes):
                s_cols = slice((c * row_tiles + j) * P, (c * row_tiles + j + 1) * P)
                m_cols = slice(c * width, (c + 1) * width)
                nc.tensor.matmul_mx(
                    out=acc,
                    lhsT=s_codes[:, s_cols].bitcast(FP8X4),
                    lhsT_scale=s_scales[:, s_cols],
                    rhs=m_codes[:, m_cols].bitcast(FP8X4),
                    rhs_scale=m_scales[:, m_cols],
                    start=(c == 0),
                    stop=(c == passes - 1),
                )

        def multiply_bb(g, h):
            acc = acc_psum.tile([P, HALF], F32, name="acc")
            for i in range(2):
                product(acc[:, 2 * P * i : 2 * P * (i + 1)], "x%d" % (g // 2), g % 2, 2, "w%d" % (2 * h + i), 2 * P, 2)
            cols = slice(h * HALF, (h + 1) * HALF)
            nc.vector.tensor_tensor(out=z[g][:, cols], in0=acc[:], in1=bias_bb[:, cols], op=ALU.add)

        def turned(q, n):
            return w[4 * q + n // 2][:, n % 2 * HALF : (n % 2 + 1) * HALF]

        def multiply_turned(q, n):
            acc = acc_psum.tile([P, HALF], F32, name="acc")
            for i in range(2):
                product(acc[:, 2 * P * i : 2 * P * (i + 1)], "w%d" % (n // 2), n % 2, 2, "x%d" % (2 * q + i), 2 * P, 2)
            return acc

        def sigmoid_turned(q, n):
            acc = multiply_turned(q, n)
            nc.scalar.activation(
                out=turned(q, n), in_=acc[:], func=FUNC.Sigmoid, scale=-1.0, bias=minus_bias_cols[:, n : n + 1]
            )

        def times_z_turned(q, n):
            acc = multiply_turned(q, n)
            nc.vector.scalar_tensor_tensor(
                out=turned(q, n), in0=acc[:], scalar=bias_cols[:, n : n + 1], in1=turned(q, n), op0=ALU.add, op1=ALU.mult
            )

        def finish_turned(g):
            for h in range(D_BB // HALF):
                if g % 2 == 0:
                    bank = acc_psum.tile([P, HALF], F32, name="acc")
                else:
                    bank = flip_psum.tile([P, HALF], F32, name="bank")
                for i in range(BLOCKS_PER_BANK):
                    block = turned(g // 4, BLOCKS_PER_BANK * h + i)[:, g % 4 * P : (g % 4 + 1) * P]
                    nc.tensor.transpose(bank[:, i * P : (i + 1) * P], block, ident[:])
                cols = slice(h * HALF, (h + 1) * HALF)
                nc.vector.tensor_tensor(out=z[g][:, cols], in0=bank[:], in1=w[RF][:, cols], op=ALU.add)
            nc.sync.dma_start(out=out[:, g, :], in_=z[g])

        rf_acc = []

        def multiply_rf(i):
            if i % 4 == 0:
                acc = acc_psum.tile([P, HALF], F32, name="acc")
                rf_acc.append(acc)
            acc = rf_acc[i // 4]
            product(acc[:, P * (i % 4) : P * (i % 4 + 1)], "rf", 0, 1, "r%d" % i, P, 4)
            if i % 4 == 3:
                cols = slice(i // 4 * HALF, (i // 4 + 1) * HALF)
                nc.vector.tensor_tensor(out=z[RF][:, cols], in0=acc[:], in1=bias_rf[:, cols], op=ALU.add)

        def sigmoid(g, cols=slice(0, D_BB)):
            nc.scalar.activation(out=w[g][:, cols], in_=z[g][:, cols], func=FUNC.Sigmoid, scale=-1.0)

        def log(g, groups=1):
            part = w_all[:, g * D_BB : (g + groups) * D_BB]
            nc.scalar.activation(out=part, in_=part, func=FUNC.Ln, bias=tiny[:])

        def tanh(g, groups=1):
            part = w_all[:, g * D_BB : (g + groups) * D_BB]
            nc.scalar.activation(out=part, in_=part, func=FUNC.Tanh, scale=-1.0)

        def times_z(g):
            nc.gpsimd.tensor_tensor(out=w[g], in0=z[g], in1=w[g], op=ALU.mult)

        def park(values, h, pool, name):
            bank = pool.tile([P, HALF], F32, name=name)
            nc.tensor.matmul(out=bank[:], lhsT=ident[:], rhs=values[:, h * HALF : (h + 1) * HALF], start=True, stop=True)
            return bank

        def with_parked(g, banks, op):
            for h in range(D_BB // HALF):
                cols = slice(h * HALF, (h + 1) * HALF)
                nc.vector.tensor_tensor(out=w[g][:, cols], in0=banks[h][:], in1=w[g][:, cols], op=op)

        def store(g, cols=slice(0, D_BB)):
            nc.sync.dma_start(out=out[:, g, cols], in_=w[g][:, cols])

        def finish(g):
            with_parked(g, rf_banks, ALU.add)
            store(g)

        first = slice(0, HALF)
        second = slice(HALF, D_BB)

        head = ["w0", "x0", "x1", "w1", "w2", "w3", "x2", "x3"]
        units = [(q, n) for q in range(2) for n in range(BLOCKS)]
        behind = {"w1": 1, "w3": 2, "x3": 13}
        for i, name in enumerate(head):
            flip(name, "SS" if name == "w1" else "VS")
            if name == "x0":
                keep_clock_up(1)
            if name == "x1":
                turn_bias()
            if i > 0:
                quantise(head[i - 1])
            if name == "x3":
                quantise("x3")
            for k in range(behind.get(name, 0)):
                sigmoid_turned(units[0][0], units[0][1])
                units.remove(units[0])
        flip("rf", "VV")
        flip("r0", "VV")
        quantise("rf")
        for q in range(2):
            log(4 * q, 4)
        load_sigmoid_table()
        for q in range(2):
            tanh(4 * q, 4)

        after = ["r%d" % i for i in range(1, 8)] + ["x4"]
        for i in range(8):
            flip(after[i], "VV")
            quantise("r%d" % i)
            if i == 4:
                for k in range(0, 4):
                    multiply_rf(k)
        flip("x5", "VV")
        quantise("x4")
        for k in range(4, 8):
            multiply_rf(k)
        sigmoid(RF)
        quantise("x5")
        for g in range(8, 12):
            multiply_bb(g, 0)
            multiply_bb(g, 1)
            sigmoid(g)
        flip("x6", "VV")
        flip("x7", "VV")
        quantise("x6")
        log(RF)
        log(8, 4)
        quantise("x7")
        load_sigmoid_table()
        tanh(RF)
        for g in range(8, 12):
            tanh(g)
        for q in range(2):
            for n in range(BLOCKS):
                times_z_turned(q, n)
        nc.vector.tensor_tensor(out=w[RF], in0=z[RF], in1=w[RF], op=ALU.mult)
        nc.gpsimd.tensor_copy(out=gate[:], in_=w[RF][:, :1])
        for g in range(8, 12):
            times_z(g)
        for g in range(12, 16):
            multiply_bb(g, 0)
            multiply_bb(g, 1)
            sigmoid(g)
        for g in range(0, 4):
            finish_turned(g)
        log(12, 4)
        for g in (8, 9):
            nc.gpsimd.tensor_tensor(out=w[g], in0=w[g], in1=w[RF], op=ALU.add)
        for g in range(4, 8):
            finish_turned(g)
            if g > 5:
                store(g + 2)
        rf_banks = [park(w[RF], h, flip_psum, "bank") for h in range(D_BB // HALF)]
        z_banks = {}
        for g in (12, 14):
            z_banks[g] = [park(z[g], h, acc_psum, "acc") for h in range(D_BB // HALF)]
        finish(10)
        finish(11)
        for g in (12, 14):
            tanh(g)
            with_parked(g, z_banks[g], ALU.mult)
            finish(g)
            tanh(g + 1)
            times_z(g + 1)
            if g == 14:
                finish(13)
        for h, cols in enumerate((first, second)):
            nc.vector.tensor_tensor(out=w[15][:, cols], in0=rf_banks[h][:], in1=w[15][:, cols], op=ALU.add)
            store(15, cols)
